import numpy as np
import ml_dtypes


def mxq(x, axis, fmt="e4m3"):
    dtype, down = {"e4m3": (ml_dtypes.float8_e4m3fn, 7), "e5m2": (ml_dtypes.float8_e5m2, 14)}[fmt]
    v = np.moveaxis(np.asarray(x, np.float32).astype(ml_dtypes.bfloat16).astype(np.float64), axis, -1)
    blocks = v.reshape(v.shape[:-1] + (-1, 32))
    amax = np.abs(blocks).max(-1, keepdims=True)
    byte = np.maximum(np.where(amax > 0, np.frexp(amax)[1] - 1 + 127, 0) - down, 1)
    scale = np.exp2(byte - 127.0)
    codes = (blocks / scale).astype(np.float32).astype(dtype).astype(np.float64)
    return np.moveaxis((codes * scale).reshape(v.shape), -1, axis)


WIDE = False


def mx_kscale(k):
    if not WIDE:
        return np.ones(k)
    levels = np.array([10, -10, 5, -5, 0])
    a = np.random.permutation(np.resize(levels, k // 512 * 4)).reshape(k // 512, 4)
    idx = np.arange(k)
    return np.exp2(a[idx // 512, idx % 128 // 32])


BF16 = ml_dtypes.bfloat16


def bf(x):
    return np.asarray(x, np.float32).astype(BF16)


def f64(x):
    return np.asarray(x).astype(np.float64)


B, G, D, H, DH, R, F, L = 1, 64, 512, 2, 256, 100, 4096, 2
S = G * G
INNER = H * DH
ROT = 2 * R
MAX_FREQ = 10.0
EPS = 1e-5


def make_freqs():
    exps = np.linspace(0.0, np.log(MAX_FREQ / 2.0) / np.log(2.0), R // 2)
    base = (2.0 ** exps) * np.pi
    t = np.linspace(-1.0, 1.0, G)
    f = np.repeat(t[:, None] * base[None, :], 2, axis=-1)
    fh = np.broadcast_to(f[:, None, :], (G, G, R))
    fw = np.broadcast_to(f[None, :, :], (G, G, R))
    return np.concatenate([fh, fw], axis=-1)


def rotate_half(u):
    u = u.reshape(u.shape[:-1] + (u.shape[-1] // 2, 2))
    return np.concatenate([-u[..., 1], u[..., 0]], axis=-1)


def apply_rot(t, cosf, sinf):
    tb = t.reshape(B, H, G, G, DH)
    tl, tr = tb[..., :ROT], tb[..., ROT:]
    tl = tl * cosf + rotate_half(tl) * sinf
    return np.concatenate([tl, tr], axis=-1).reshape(B, H, S, DH)


def to_heads(t):
    return t.reshape(B, S, H, DH).transpose(0, 2, 1, 3)


def setup_inputs():
    s = mx_kscale(D)
    return {'x_grid': bf(np.random.standard_normal((B, S, D))),
            'ln_g': bf((1.0 + 0.1 * np.random.standard_normal(D)) * s),
            'ln_b': bf(0.1 * np.random.standard_normal(D) * s),
            'w_qk': bf(np.random.standard_normal((D, 2 * INNER)) * 1.5 / np.sqrt(D) / s[:, None])}


def reference(x_grid, ln_g, ln_b, w_qk):
    x = f64(x_grid)
    mu = np.mean(x, axis=-1, keepdims=True)
    var = np.mean(np.square(x - mu), axis=-1, keepdims=True)
    xn = (x - mu) / np.sqrt(var + EPS) * f64(ln_g) + f64(ln_b)
    qk = mxq(xn, 2, 'e4m3') @ mxq(f64(w_qk), 0, 'e4m3')
    q, k = to_heads(qk[..., :INNER]), to_heads(qk[..., INNER:])
    freqs = make_freqs()
    cosf, sinf = np.cos(freqs)[None, None], np.sin(freqs)[None, None]
    return apply_rot(q, cosf, sinf), apply_rot(k, cosf, sinf)

@@ -1,0 +1,348 @@
+import math
+from contextlib import ExitStack
+
+import concourse.masks as masks
+import concourse.mybir as mybir
+
+F32 = mybir.dt.float32
+BF16 = mybir.dt.bfloat16
+I32 = mybir.dt.int32
+U32 = mybir.dt.uint32
+U8 = mybir.dt.uint8
+FP8X4 = mybir.dt.float8_e4m3fn_x4
+ALU = mybir.AluOpType
+ACT = mybir.ActivationFunctionType
+
+P = 128
+PACK = 4
+D = P * PACK
+TOKENS = 4096
+GRID = 64
+HEADS = 2
+DH = 256
+INNER = HEADS * DH
+ROT = 200
+HALF = ROT // 2
+FREQS = HALF // 2
+PLAIN = DH - ROT
+EPS = 1e-5
+
+BLOCKS = 4
+LANES = 8
+GROUP = 2
+GROUPS = BLOCKS * LANES // GROUP
+GROUP_TOKENS = GROUP * P
+SLOTS = BLOCKS + LANES
+
+FLOPS = 2 * TOKENS * D * 2 * INNER
+
+
+def build_rotary_tables(nc, keep, work):
+    part = work.tile([P, 1], I32)
+    nc.gpsimd.iota(part[:], pattern=[[0, 1]], base=0, channel_multiplier=1)
+    offsets = work.tile([P, SLOTS], I32)
+    nc.gpsimd.iota(offsets[:, 0:BLOCKS], pattern=[[GRID // BLOCKS, BLOCKS]], base=0, channel_multiplier=0)
+    nc.gpsimd.iota(offsets[:, BLOCKS:SLOTS], pattern=[[1, LANES]], base=0, channel_multiplier=0)
+    row_base = work.tile([P, 1], I32)
+    nc.vector.tensor_single_scalar(out=row_base[:], in_=part[:], scalar=3, op=ALU.arith_shift_right)
+    col_base = work.tile([P, 1], I32)
+    nc.vector.tensor_scalar(
+        out=col_base[:], in0=part[:], scalar1=7, scalar2=3,
+        op0=ALU.bitwise_and, op1=ALU.logical_shift_left,
+    )
+    half_t = work.tile([P, SLOTS], F32)
+    nc.vector.tensor_scalar(
+        out=half_t[:, 0:BLOCKS], in0=offsets[:, 0:BLOCKS], scalar1=row_base[:, 0:1],
+        scalar2=1.0 / (GRID - 1), op0=ALU.add, op1=ALU.mult,
+    )
+    nc.vector.tensor_scalar(
+        out=half_t[:, BLOCKS:SLOTS], in0=offsets[:, BLOCKS:SLOTS], scalar1=col_base[:, 0:1],
+        scalar2=1.0 / (GRID - 1), op0=ALU.add, op1=ALU.mult,
+    )
+    nc.vector.tensor_scalar_add(out=half_t[:], in0=half_t[:], scalar1=-0.5)
+
+    beta = work.tile([P, FREQS], F32)
+    nc.vector.memset(beta[:, 0:1], 1.0)
+    ratio = 5.0 ** (1.0 / (FREQS - 1))
+    have = 1
+    while have < FREQS:
+        more = min(have, FREQS - have)
+        nc.vector.tensor_scalar_mul(
+            out=beta[:, have : have + more], in0=beta[:, 0:more], scalar1=ratio**have
+        )
+        have += more
+
+    shape = [P, SLOTS, FREQS]
+    turns = work.tile([P, 2, SLOTS, FREQS], F32)
+    nc.vector.tensor_tensor(
+        out=turns[:, 0], in0=half_t[:].unsqueeze(2).to_broadcast(shape),
+        in1=beta[:].unsqueeze(1).to_broadcast(shape), op=ALU.mult,
+    )
+    nc.vector.tensor_scalar_add(out=turns[:, 1], in0=turns[:, 0], scalar1=-0.25)
+    whole = work.tile([P, 2, SLOTS, FREQS], I32)
+    nc.vector.tensor_copy(out=whole[:], in_=turns[:])
+    rest = work.tile([P, 2, SLOTS, FREQS], F32)
+    nc.vector.tensor_tensor(out=rest[:], in0=turns[:], in1=whole[:], op=ALU.subtract)
+    half_sin = work.tile([P, 2, SLOTS, FREQS], F32)
+    nc.scalar.activation(out=half_sin[:], in_=rest[:], func=ACT.Sin, scale=math.pi)
+    square = work.tile([P, 2, SLOTS, FREQS], F32)
+    nc.gpsimd.tensor_tensor(out=square[:], in0=half_sin[:], in1=half_sin[:], op=ALU.mult)
+
+    cos_tab = keep.tile([P, SLOTS, HALF], F32)
+    sin_tab = keep.tile([P, SLOTS, HALF], F32)
+
+    def finish(table_slots, squares, sign):
+        count = squares.shape[1]
+        nc.gpsimd.tensor_scalar(
+            out=table_slots.rearrange("p s (j e) -> p s j e", e=2),
+            in0=squares.unsqueeze(3).to_broadcast([P, count, FREQS, 2]),
+            scalar1=-2.0 * sign, scalar2=sign, op0=ALU.mult, op1=ALU.add,
+        )
+
+    finish(cos_tab[:], square[:, 0], 1.0)
+    finish(sin_tab[:, 0:LANES], square[:, 1, BLOCKS:SLOTS], 1.0)
+    finish(sin_tab[:, LANES:SLOTS], square[:, 1, 0:BLOCKS], -1.0)
+    return cos_tab, sin_tab
+
+
+def load_gain_and_bias(nc, keep, work, psum, ident, ln_g, ln_b):
+    rows = work.tile([P, P], BF16)
+    nc.vector.memset(rows[:], 0.0)
+    nc.sync.dma_start(out=rows[0:PACK, :], in_=ln_g.rearrange("(t p) -> t p", p=P))
+    nc.sync.dma_start(out=rows[PACK : 2 * PACK, :], in_=ln_b.rearrange("(t p) -> t p", p=P))
+    rows32 = work.tile([P, P], F32)
+    nc.vector.tensor_copy(out=rows32[:], in_=rows[:])
+    columns = psum.tile([P, P], F32, tag="zt")
+    nc.tensor.transpose(out=columns[:], in_=rows32[:], identity=ident[:])
+    gain_bias = keep.tile([P, 2 * PACK], F32)
+    nc.vector.tensor_copy(out=gain_bias[:], in_=columns[:, 0 : 2 * PACK])
+    return gain_bias
+
+
+def quantise_weights(nc, keep, work, w_qk):
+    cols = 2 * INNER
+    raw = work.tile([P, PACK, cols], BF16)
+    nc.sync.dma_start(out=raw[:], in_=w_qk.rearrange("(t p) n -> p t n", p=P))
+    grouped = work.tile([P, cols, PACK], BF16, align_bytes=64)
+    nc.vector.tensor_copy(out=grouped[:], in_=raw[:].rearrange("p t n -> p n t"))
+    codes = keep.tile([P, cols], U32, align_bytes=64)
+    scales = keep.tile([P, cols], U8, align_bytes=64)
+    nc.vector.quantize_mx(
+        out=codes[:].bitcast(FP8X4), scales=scales[:], in_=grouped[:].rearrange("p n t -> p (n t)")
+    )
+
+    plain_grouped = work.tile([P, DH, PACK], BF16, align_bytes=64)
+    nc.vector.memset(plain_grouped[:], 0.0)
+    nc.vector.tensor_copy(
+        out=plain_grouped[:, 0 : 2 * HEADS * PLAIN, :].rearrange("p (g c) t -> p g c t", c=PLAIN),
+        in_=raw[:].rearrange("p t (g c) -> p g c t", c=DH)[:, :, ROT:DH, :],
+    )
+    plain_codes = keep.tile([P, DH], U32, align_bytes=64)
+    plain_scales = keep.tile([P, DH], U8, align_bytes=64)
+    nc.vector.quantize_mx(
+        out=plain_codes[:].bitcast(FP8X4), scales=plain_scales[:],
+        in_=plain_grouped[:].rearrange("p n t -> p (n t)"),
+    )
+    return codes, scales, plain_codes, plain_scales
+
+
+def tile_transformerencoderlayer_pa_t_kernel(tc, x_grid, ln_g, ln_b, w_qk, out_0, out_1):
+    nc = tc.nc
+    x_view = x_grid.rearrange("o (a p l) k -> p (o a) (l k)", a=BLOCKS, p=P, l=LANES)
+    out_views = [
+        out.rearrange("o h (a p l) c -> p (o h) a (l c)", a=BLOCKS, p=P, l=LANES)
+        for out in (out_0, out_1)
+    ]
+
+    with ExitStack() as ctx:
+        keep = ctx.enter_context(tc.tile_pool(name="keep", bufs=1))
+        work = ctx.enter_context(tc.tile_pool(name="work", bufs=1))
+        stats = ctx.enter_context(tc.tile_pool(name="stats", bufs=6))
+        stage = ctx.enter_context(tc.tile_pool(name="stage", bufs=3))
+        results = ctx.enter_context(tc.tile_pool(name="results", bufs=4))
+        zt_psum = ctx.enter_context(tc.psum_pool(name="zt_psum", bufs=2))
+        u_psum = ctx.enter_context(tc.psum_pool(name="u_psum", bufs=4))
+        plain_psum = ctx.enter_context(tc.psum_pool(name="plain_psum", bufs=2))
+
+        def block_and_lane(g):
+            return g // (LANES // GROUP), GROUP * (g % (LANES // GROUP))
+
+        x_sb = keep.tile([P, GROUPS, GROUP, D], BF16)
+
+        def load_x(g):
+            a, lane = block_and_lane(g)
+            nc.sync.dma_start(
+                out=x_sb[:, g].rearrange("p s k -> p (s k)"),
+                in_=x_view[:, a, lane * D : (lane + GROUP) * D],
+            )
+
+        load_x(0)
+        ident = keep.tile([P, P], F32)
+        masks.make_identity(nc, ident[:])
+        gain_bias = load_gain_and_bias(nc, keep, work, zt_psum, ident, ln_g, ln_b)
+        load_x(1)
+        w_codes, w_scales, plain_codes, plain_scales = quantise_weights(nc, keep, work, w_qk)
+        for g in range(2, GROUPS):
+            load_x(g)
+        cos_tab, sin_tab = build_rotary_tables(nc, keep, work)
+
+        eps = keep.tile([P, 1], F32)
+        nc.vector.memset(eps[:], EPS)
+        discard = keep.tile([P, D], BF16)
+        neg_means, scales_shifts, z_tiles, xn_operands, u_banks, plain_banks = {}, {}, {}, {}, {}, {}
+
+        def sum_features(g):
+            total = stats.tile([P, GROUP], F32)
+            for s in range(GROUP):
+                nc.scalar.activation(
+                    out=discard[:], in_=x_sb[:, g, s], func=ACT.Copy, accum_out=total[:, s : s + 1]
+                )
+            neg_mean = stats.tile([P, GROUP], F32)
+            nc.vector.tensor_scalar_mul(out=neg_mean[:], in0=total[:], scalar1=-1.0 / D)
+            neg_means[g] = neg_mean
+
+        def sum_squared_deviations(g):
+            neg_mean = neg_means[g]
+            squares = stats.tile([P, GROUP], F32)
+            for s in range(GROUP):
+                nc.scalar.activation(
+                    out=discard[:], in_=x_sb[:, g, s], func=ACT.Square,
+                    bias=neg_mean[:, s : s + 1], accum_out=squares[:, s : s + 1],
+                )
+            std = stats.tile([P, GROUP], F32)
+            nc.scalar.activation(out=std[:], in_=squares[:], func=ACT.Sqrt, scale=1.0 / D, bias=eps[:, 0:1])
+            rstd = stats.tile([P, GROUP], F32)
+            nc.vector.reciprocal(out=rstd[:], in_=std[:])
+            shift = stats.tile([P, GROUP], F32)
+            nc.vector.tensor_mul(out=shift[:], in0=neg_mean[:], in1=rstd[:])
+            scales_shifts[g] = (rstd, shift)
+
+        def normalise_and_transpose(g):
+            rstd, shift = scales_shifts[g]
+            z = stage.tile([P, GROUP, D], F32)
+            for s in range(GROUP):
+                nc.scalar.activation(
+                    out=z[:, s], in_=x_sb[:, g, s], func=ACT.Identity,
+                    scale=rstd[:, s : s + 1], bias=shift[:, s : s + 1],
+                )
+            banks = []
+            for half in range(2):
+                zt = zt_psum.tile([P, 2, GROUP_TOKENS], F32, tag="zt")
+                for i in range(2):
+                    t = 2 * half + i
+                    for s in range(GROUP):
+                        nc.tensor.transpose(
+                            out=zt[:, i, s * P : (s + 1) * P], in_=z[:, s, t * P : (t + 1) * P],
+                            identity=ident[:],
+                        )
+                banks.append(zt)
+            z_tiles[g] = banks
+
+        def scale_shift_and_quantise(g):
+            planes = stage.tile([P, PACK, GROUP_TOKENS], BF16)
+            for half in range(2):
+                for i in range(2):
+                    t = 2 * half + i
+                    nc.scalar.activation(
+                        out=planes[:, t], in_=z_tiles[g][half][:, i], func=ACT.Identity,
+                        scale=gain_bias[:, t : t + 1], bias=gain_bias[:, PACK + t : PACK + t + 1],
+                    )
+            grouped = stage.tile([P, GROUP_TOKENS, PACK], BF16, align_bytes=64)
+            nc.vector.tensor_copy(out=grouped[:], in_=planes[:].rearrange("p t w -> p w t"))
+            codes = stage.tile([P, GROUP_TOKENS], U32, align_bytes=64)
+            scales = stage.tile([P, GROUP_TOKENS], U8, align_bytes=64)
+            nc.vector.quantize_mx(
+                out=codes[:].bitcast(FP8X4), scales=scales[:],
+                in_=grouped[:].rearrange("p w t -> p (w t)"),
+            )
+            xn_operands[g] = (codes, scales)
+
+        def project(g, s, qk):
+            codes, scales = xn_operands[g]
+            tokens = slice(s * P, (s + 1) * P)
+            columns = slice(qk * INNER, (qk + 1) * INNER)
+            u = u_psum.tile([P, INNER], F32)
+            nc.tensor.matmul_mx(
+                out=u[:],
+                lhsT=codes[:, tokens].bitcast(FP8X4), lhsT_scale=scales[:, tokens],
+                rhs=w_codes[:, columns].bitcast(FP8X4), rhs_scale=w_scales[:, columns],
+                start=True, stop=True,
+            )
+            u_banks[(g, s, qk)] = u
+
+        def project_plain(g):
+            codes, scales = xn_operands[g]
+            plain = plain_psum.tile([P, GROUP, DH], F32)
+            for s in range(GROUP):
+                tokens = slice(s * P, (s + 1) * P)
+                nc.tensor.matmul_mx(
+                    out=plain[:, s],
+                    lhsT=codes[:, tokens].bitcast(FP8X4), lhsT_scale=scales[:, tokens],
+                    rhs=plain_codes[:].bitcast(FP8X4), rhs_scale=plain_scales[:],
+                    start=True, stop=True,
+                )
+            plain_banks[g] = plain
+
+        def rotate_and_store(g):
+            a, lane = block_and_lane(g)
+            y = results.tile([P, 2, HEADS, GROUP, DH], F32)
+            partner = results.tile([P, 2, HEADS, GROUP, ROT], F32)
+            both_heads = [P, HEADS, 2, HALF]
+            for s in range(GROUP):
+                l = lane + s
+                cosines = cos_tab[:, a : BLOCKS + l + 1 : BLOCKS + l - a]
+                sines = sin_tab[:, l : LANES + a + 1 : LANES + a - l]
+                for qk in range(2):
+                    u = u_banks[(g, s, qk)][:].rearrange("p (h c) -> p h c", h=HEADS)[:, :, 0:ROT]
+                    nc.vector.tensor_tensor(
+                        out=y[:, qk, :, s, 0:ROT].rearrange("p h (f c) -> p h f c", f=2),
+                        in0=u.rearrange("p h (f c) -> p h f c", f=2),
+                        in1=cosines.unsqueeze(1).to_broadcast(both_heads),
+                        op=ALU.mult,
+                    )
+                    nc.vector.tensor_tensor(
+                        out=partner[:, qk, :, s].rearrange("p h (e i) -> p h e i", e=2),
+                        in0=u.rearrange("p h (i e) -> p h e i", e=2),
+                        in1=sines.unsqueeze(1).to_broadcast(both_heads),
+                        op=ALU.mult,
+                    )
+                    if g + 1 < GROUPS:
+                        project(g + 1, s, qk)
+            nc.scalar.copy(
+                out=y[:].rearrange("p q h s c -> p s (q h) c")[:, :, :, ROT:DH],
+                in_=plain_banks[g][:, :, 0 : 2 * HEADS * PLAIN].rearrange("p s (g c) -> p s g c", c=PLAIN),
+            )
+            if g + 1 < GROUPS:
+                project_plain(g + 1)
+            y_rows = y[:].rearrange("p q h s c -> p (q h s) c")
+            partner_rows = partner[:].rearrange("p q h s c -> p (q h s) c")
+            nc.gpsimd.tensor_tensor(
+                out=y_rows[:, :, HALF:ROT], in0=y_rows[:, :, HALF:ROT],
+                in1=partner_rows[:, :, 0:HALF], op=ALU.add,
+            )
+            nc.gpsimd.tensor_tensor(
+                out=y_rows[:, :, 0:HALF], in0=y_rows[:, :, 0:HALF],
+                in1=partner_rows[:, :, HALF:ROT], op=ALU.add,
+            )
+            for qk in range(2):
+                nc.sync.dma_start(
+                    out=out_views[qk][:, :, a, lane * DH : (lane + GROUP) * DH],
+                    in_=y[:, qk].rearrange("p h s c -> p h (s c)"),
+                )
+
+        for k in range(GROUPS + 4):
+            if k < GROUPS:
+                sum_features(k)
+            if 0 <= k - 1 < GROUPS:
+                sum_squared_deviations(k - 1)
+            if 0 <= k - 2 < GROUPS:
+                normalise_and_transpose(k - 2)
+            if 0 <= k - 3 < GROUPS:
+                scale_shift_and_quantise(k - 3)
+            if k == 3:
+                for s in range(GROUP):
+                    for qk in range(2):
+                        project(0, s, qk)
+                project_plain(0)
+            if 0 <= k - 4 < GROUPS:
+                rotate_and_store(k - 4)

@@ -316,11 +316,11 @@ def tile_transformerencoderlayer_pa_t_kernel(tc, x_grid, ln_g, ln_b, w_qk, out_0
                 project_plain(g + 1)
             y_rows = y[:].rearrange("p q h s c -> p (q h s) c")
             partner_rows = partner[:].rearrange("p q h s c -> p (q h s) c")
-            nc.gpsimd.tensor_tensor(
+            nc.vector.tensor_tensor(
                 out=y_rows[:, :, HALF:ROT], in0=y_rows[:, :, HALF:ROT],
                 in1=partner_rows[:, :, 0:HALF], op=ALU.add,
             )
-            nc.gpsimd.tensor_tensor(
+            nc.vector.tensor_tensor(
                 out=y_rows[:, :, 0:HALF], in0=y_rows[:, :, 0:HALF],
                 in1=partner_rows[:, :, HALF:ROT], op=ALU.add,
             )

@@ -37,7 +37,7 @@ SLOTS = BLOCKS + LANES
 FLOPS = 2 * TOKENS * D * 2 * INNER
 
 
-def build_rotary_tables(nc, keep, work):
+def rotary_turns(nc, work):
     part = work.tile([P, 1], I32)
     nc.gpsimd.iota(part[:], pattern=[[0, 1]], base=0, channel_multiplier=1)
     offsets = work.tile([P, SLOTS], I32)
@@ -83,17 +83,18 @@ def build_rotary_tables(nc, keep, work):
     nc.vector.tensor_copy(out=whole[:], in_=turns[:])
     rest = work.tile([P, 2, SLOTS, FREQS], F32)
     nc.vector.tensor_tensor(out=rest[:], in0=turns[:], in1=whole[:], op=ALU.subtract)
-    half_sin = work.tile([P, 2, SLOTS, FREQS], F32)
-    nc.scalar.activation(out=half_sin[:], in_=rest[:], func=ACT.Sin, scale=math.pi)
-    square = work.tile([P, 2, SLOTS, FREQS], F32)
-    nc.gpsimd.tensor_tensor(out=square[:], in0=half_sin[:], in1=half_sin[:], op=ALU.mult)
+    return rest
 
+
+def rotary_tables(nc, keep, work, half_sin):
+    square = work.tile([P, 2, SLOTS, FREQS], F32)
+    nc.vector.tensor_tensor(out=square[:], in0=half_sin[:], in1=half_sin[:], op=ALU.mult)
     cos_tab = keep.tile([P, SLOTS, HALF], F32)
     sin_tab = keep.tile([P, SLOTS, HALF], F32)
 
     def finish(table_slots, squares, sign):
         count = squares.shape[1]
-        nc.gpsimd.tensor_scalar(
+        nc.vector.tensor_scalar(
             out=table_slots.rearrange("p s (j e) -> p s j e", e=2),
             in0=squares.unsqueeze(3).to_broadcast([P, count, FREQS, 2]),
             scalar1=-2.0 * sign, scalar2=sign, op0=ALU.mult, op1=ALU.add,
@@ -105,37 +106,20 @@ def build_rotary_tables(nc, keep, work):
     return cos_tab, sin_tab
 
 
-def load_gain_and_bias(nc, keep, work, psum, ident, ln_g, ln_b):
-    rows = work.tile([P, P], BF16)
-    nc.vector.memset(rows[:], 0.0)
-    nc.sync.dma_start(out=rows[0:PACK, :], in_=ln_g.rearrange("(t p) -> t p", p=P))
-    nc.sync.dma_start(out=rows[PACK : 2 * PACK, :], in_=ln_b.rearrange("(t p) -> t p", p=P))
-    rows32 = work.tile([P, P], F32)
-    nc.vector.tensor_copy(out=rows32[:], in_=rows[:])
-    columns = psum.tile([P, P], F32, tag="zt")
-    nc.tensor.transpose(out=columns[:], in_=rows32[:], identity=ident[:])
-    gain_bias = keep.tile([P, 2 * PACK], F32)
-    nc.vector.tensor_copy(out=gain_bias[:], in_=columns[:, 0 : 2 * PACK])
-    return gain_bias
-
-
-def quantise_weights(nc, keep, work, w_qk):
+def quantise_weights(nc, keep, work, raw):
     cols = 2 * INNER
-    raw = work.tile([P, PACK, cols], BF16)
-    nc.sync.dma_start(out=raw[:], in_=w_qk.rearrange("(t p) n -> p t n", p=P))
     grouped = work.tile([P, cols, PACK], BF16, align_bytes=64)
     nc.vector.tensor_copy(out=grouped[:], in_=raw[:].rearrange("p t n -> p n t"))
     codes = keep.tile([P, cols], U32, align_bytes=64)
     scales = keep.tile([P, cols], U8, align_bytes=64)
-    nc.vector.quantize_mx(
-        out=codes[:].bitcast(FP8X4), scales=scales[:], in_=grouped[:].rearrange("p n t -> p (n t)")
-    )
-
     plain_grouped = work.tile([P, DH, PACK], BF16, align_bytes=64)
     nc.vector.memset(plain_grouped[:], 0.0)
     nc.vector.tensor_copy(
         out=plain_grouped[:, 0 : 2 * HEADS * PLAIN, :].rearrange("p (g c) t -> p g c t", c=PLAIN),
         in_=raw[:].rearrange("p t (g c) -> p g c t", c=DH)[:, :, ROT:DH, :],
+    )
+    nc.vector.quantize_mx(
+        out=codes[:].bitcast(FP8X4), scales=scales[:], in_=grouped[:].rearrange("p n t -> p (n t)")
     )
     plain_codes = keep.tile([P, DH], U32, align_bytes=64)
     plain_scales = keep.tile([P, DH], U8, align_bytes=64)
@@ -157,12 +141,13 @@ def tile_transformerencoderlayer_pa_t_kernel(tc, x_grid, ln_g, ln_b, w_qk, out_0
     with ExitStack() as ctx:
         keep = ctx.enter_context(tc.tile_pool(name="keep", bufs=1))
         work = ctx.enter_context(tc.tile_pool(name="work", bufs=1))
-        stats = ctx.enter_context(tc.tile_pool(name="stats", bufs=6))
+        stats = ctx.enter_context(tc.tile_pool(name="stats", bufs=4))
         stage = ctx.enter_context(tc.tile_pool(name="stage", bufs=3))
-        results = ctx.enter_context(tc.tile_pool(name="results", bufs=4))
+        results = ctx.enter_context(tc.tile_pool(name="results", bufs=3))
         zt_psum = ctx.enter_context(tc.psum_pool(name="zt_psum", bufs=2))
         u_psum = ctx.enter_context(tc.psum_pool(name="u_psum", bufs=4))
         plain_psum = ctx.enter_context(tc.psum_pool(name="plain_psum", bufs=2))
+        ctx.enter_context(tc.manual_schedule())
 
         def block_and_lane(g):
             return g // (LANES // GROUP), GROUP * (g % (LANES // GROUP))
@@ -176,20 +161,34 @@ def tile_transformerencoderlayer_pa_t_kernel(tc, x_grid, ln_g, ln_b, w_qk, out_0
                 in_=x_view[:, a, lane * D : (lane + GROUP) * D],
             )
 
+        gb_rows = work.tile([P, P], BF16)
+        nc.vector.memset(gb_rows[:], 0.0)
+        w_raw = work.tile([P, PACK, 2 * INNER], BF16)
         load_x(0)
-        ident = keep.tile([P, P], F32)
-        masks.make_identity(nc, ident[:])
-        gain_bias = load_gain_and_bias(nc, keep, work, zt_psum, ident, ln_g, ln_b)
+        nc.sync.dma_start(out=gb_rows[0:PACK, :], in_=ln_g.rearrange("(t p) -> t p", p=P))
+        nc.sync.dma_start(out=gb_rows[PACK : 2 * PACK, :], in_=ln_b.rearrange("(t p) -> t p", p=P))
         load_x(1)
-        w_codes, w_scales, plain_codes, plain_scales = quantise_weights(nc, keep, work, w_qk)
+        nc.sync.dma_start(out=w_raw[:], in_=w_qk.rearrange("(t p) n -> p t n", p=P))
         for g in range(2, GROUPS):
             load_x(g)
-        cos_tab, sin_tab = build_rotary_tables(nc, keep, work)
 
-        eps = keep.tile([P, 1], F32)
-        nc.vector.memset(eps[:], EPS)
+        minus_half = keep.tile([P, GROUP], F32)
+        nc.vector.memset(minus_half[:], -0.5)
+        warm = work.tile([P, 1], F32)
+        nc.scalar.activation(out=warm[:], in_=minus_half[:, 0:1], func=ACT.Sin)
+        rest = rotary_turns(nc, work)
+        ident = keep.tile([P, P], F32)
+        masks.make_identity(nc, ident[:])
+        gb_rows32 = work.tile([P, P], F32)
+        nc.vector.tensor_copy(out=gb_rows32[:], in_=gb_rows[:])
+        gb_columns = zt_psum.tile([P, P], F32, tag="zt")
+        nc.tensor.transpose(out=gb_columns[:], in_=gb_rows32[:], identity=ident[:])
+        gain_bias = keep.tile([P, 2 * PACK], F32)
+        nc.vector.tensor_copy(out=gain_bias[:], in_=gb_columns[:, 0 : 2 * PACK])
+
         discard = keep.tile([P, D], BF16)
-        neg_means, scales_shifts, z_tiles, xn_operands, u_banks, plain_banks = {}, {}, {}, {}, {}, {}
+        neg_means, z_tiles, zt_banks, xn_grouped, xn_operands = {}, {}, {}, {}, {}
+        u_banks, plain_banks, y_tiles, partner_tiles = {}, {}, {}, {}
 
         def sum_features(g):
             total = stats.tile([P, GROUP], F32)
@@ -198,10 +197,12 @@ def tile_transformerencoderlayer_pa_t_kernel(tc, x_grid, ln_g, ln_b, w_qk, out_0
                     out=discard[:], in_=x_sb[:, g, s], func=ACT.Copy, accum_out=total[:, s : s + 1]
                 )
             neg_mean = stats.tile([P, GROUP], F32)
-            nc.vector.tensor_scalar_mul(out=neg_mean[:], in0=total[:], scalar1=-1.0 / D)
+            nc.gpsimd.tensor_scalar(
+                out=neg_mean[:], in0=total[:], scalar1=-1.0 / D, scalar2=0.0, op0=ALU.mult, op1=ALU.add
+            )
             neg_means[g] = neg_mean
 
-        def sum_squared_deviations(g):
+        def normalise(g):
             neg_mean = neg_means[g]
             squares = stats.tile([P, GROUP], F32)
             for s in range(GROUP):
@@ -209,22 +210,24 @@ def tile_transformerencoderlayer_pa_t_kernel(tc, x_grid, ln_g, ln_b, w_qk, out_0
                     out=discard[:], in_=x_sb[:, g, s], func=ACT.Square,
                     bias=neg_mean[:, s : s + 1], accum_out=squares[:, s : s + 1],
                 )
-            std = stats.tile([P, GROUP], F32)
-            nc.scalar.activation(out=std[:], in_=squares[:], func=ACT.Sqrt, scale=1.0 / D, bias=eps[:, 0:1])
+            var_eps = stats.tile([P, GROUP], F32)
+            nc.gpsimd.tensor_scalar(
+                out=var_eps[:], in0=squares[:], scalar1=1.0 / D, scalar2=EPS, op0=ALU.mult, op1=ALU.add
+            )
             rstd = stats.tile([P, GROUP], F32)
-            nc.vector.reciprocal(out=rstd[:], in_=std[:])
+            nc.gpsimd.tensor_tensor(out=rstd[:], in0=var_eps[:], in1=minus_half[:], op=ALU.pow)
             shift = stats.tile([P, GROUP], F32)
-            nc.vector.tensor_mul(out=shift[:], in0=neg_mean[:], in1=rstd[:])
-            scales_shifts[g] = (rstd, shift)
-
-        def normalise_and_transpose(g):
-            rstd, shift = scales_shifts[g]
+            nc.gpsimd.tensor_tensor(out=shift[:], in0=neg_mean[:], in1=rstd[:], op=ALU.mult)
             z = stage.tile([P, GROUP, D], F32)
             for s in range(GROUP):
-                nc.scalar.activation(
-                    out=z[:, s], in_=x_sb[:, g, s], func=ACT.Identity,
-                    scale=rstd[:, s : s + 1], bias=shift[:, s : s + 1],
+                nc.gpsimd.tensor_scalar(
+                    out=z[:, s], in0=x_sb[:, g, s], scalar1=rstd[:, s : s + 1],
+                    scalar2=shift[:, s : s + 1], op0=ALU.mult, op1=ALU.add,
                 )
+            z_tiles[g] = z
+
+        def transpose(g):
+            z = z_tiles[g]
             banks = []
             for half in range(2):
                 zt = zt_psum.tile([P, 2, GROUP_TOKENS], F32, tag="zt")
@@ -236,42 +239,44 @@ def tile_transformerencoderlayer_pa_t_kernel(tc, x_grid, ln_g, ln_b, w_qk, out_0
                             identity=ident[:],
                         )
                 banks.append(zt)
-            z_tiles[g] = banks
+            zt_banks[g] = banks
 
-        def scale_shift_and_quantise(g):
+        def scale_shift_and_regroup(g):
             planes = stage.tile([P, PACK, GROUP_TOKENS], BF16)
             for half in range(2):
                 for i in range(2):
                     t = 2 * half + i
                     nc.scalar.activation(
-                        out=planes[:, t], in_=z_tiles[g][half][:, i], func=ACT.Identity,
+                        out=planes[:, t], in_=zt_banks[g][half][:, i], func=ACT.Identity,
                         scale=gain_bias[:, t : t + 1], bias=gain_bias[:, PACK + t : PACK + t + 1],
                     )
             grouped = stage.tile([P, GROUP_TOKENS, PACK], BF16, align_bytes=64)
-            nc.vector.tensor_copy(out=grouped[:], in_=planes[:].rearrange("p t w -> p w t"))
+            nc.scalar.copy(out=grouped[:], in_=planes[:].rearrange("p t w -> p w t"))
+            xn_grouped[g] = grouped
+
+        def quantise(g):
             codes = stage.tile([P, GROUP_TOKENS], U32, align_bytes=64)
             scales = stage.tile([P, GROUP_TOKENS], U8, align_bytes=64)
             nc.vector.quantize_mx(
                 out=codes[:].bitcast(FP8X4), scales=scales[:],
-                in_=grouped[:].rearrange("p w t -> p (w t)"),
+                in_=xn_grouped[g][:].rearrange("p w t -> p (w t)"),
             )
             xn_operands[g] = (codes, scales)
 
-        def project(g, s, qk):
+        def project(g):
             codes, scales = xn_operands[g]
-            tokens = slice(s * P, (s + 1) * P)
-            columns = slice(qk * INNER, (qk + 1) * INNER)
-            u = u_psum.tile([P, INNER], F32)
-            nc.tensor.matmul_mx(
-                out=u[:],
-                lhsT=codes[:, tokens].bitcast(FP8X4), lhsT_scale=scales[:, tokens],
-                rhs=w_codes[:, columns].bitcast(FP8X4), rhs_scale=w_scales[:, columns],
-                start=True, stop=True,
-            )
-            u_banks[(g, s, qk)] = u
-
-        def project_plain(g):
-            codes, scales = xn_operands[g]
+            for s in range(GROUP):
+                tokens = slice(s * P, (s + 1) * P)
+                for qk in range(2):
+                    columns = slice(qk * INNER, (qk + 1) * INNER)
+                    u = u_psum.tile([P, INNER], F32)
+                    nc.tensor.matmul_mx(
+                        out=u[:],
+                        lhsT=codes[:, tokens].bitcast(FP8X4), lhsT_scale=scales[:, tokens],
+                        rhs=w_codes[:, columns].bitcast(FP8X4), rhs_scale=w_scales[:, columns],
+                        start=True, stop=True,
+                    )
+                    u_banks[(g, s, qk)] = u
             plain = plain_psum.tile([P, GROUP, DH], F32)
             for s in range(GROUP):
                 tokens = slice(s * P, (s + 1) * P)
@@ -283,7 +288,7 @@ def tile_transformerencoderlayer_pa_t_kernel(tc, x_grid, ln_g, ln_b, w_qk, out_0
                 )
             plain_banks[g] = plain
 
-        def rotate_and_store(g):
+        def multiply_by_tables(g):
             a, lane = block_and_lane(g)
             y = results.tile([P, 2, HEADS, GROUP, DH], F32)
             partner = results.tile([P, 2, HEADS, GROUP, ROT], F32)
@@ -306,16 +311,14 @@ def tile_transformerencoderlayer_pa_t_kernel(tc, x_grid, ln_g, ln_b, w_qk, out_0
                         in1=sines.unsqueeze(1).to_broadcast(both_heads),
                         op=ALU.mult,
                     )
-                    if g + 1 < GROUPS:
-                        project(g + 1, s, qk)
-            nc.scalar.copy(
-                out=y[:].rearrange("p q h s c -> p s (q h) c")[:, :, :, ROT:DH],
-                in_=plain_banks[g][:, :, 0 : 2 * HEADS * PLAIN].rearrange("p s (g c) -> p s g c", c=PLAIN),
-            )
-            if g + 1 < GROUPS:
-                project_plain(g + 1)
+            y_tiles[g] = y
+            partner_tiles[g] = partner
+
+        def add_and_store(g):
+            a, lane = block_and_lane(g)
+            y = y_tiles[g]
             y_rows = y[:].rearrange("p q h s c -> p (q h s) c")
-            partner_rows = partner[:].rearrange("p q h s c -> p (q h s) c")
+            partner_rows = partner_tiles[g][:].rearrange("p q h s c -> p (q h s) c")
             nc.vector.tensor_tensor(
                 out=y_rows[:, :, HALF:ROT], in0=y_rows[:, :, HALF:ROT],
                 in1=partner_rows[:, :, 0:HALF], op=ALU.add,
@@ -324,25 +327,37 @@ def tile_transformerencoderlayer_pa_t_kernel(tc, x_grid, ln_g, ln_b, w_qk, out_0
                 out=y_rows[:, :, 0:HALF], in0=y_rows[:, :, 0:HALF],
                 in1=partner_rows[:, :, HALF:ROT], op=ALU.add,
             )
+            nc.scalar.copy(
+                out=y[:].rearrange("p q h s c -> p s (q h) c")[:, :, :, ROT:DH],
+                in_=plain_banks[g][:, :, 0 : 2 * HEADS * PLAIN].rearrange("p s (g c) -> p s g c", c=PLAIN),
+            )
             for qk in range(2):
                 nc.sync.dma_start(
                     out=out_views[qk][:, :, a, lane * DH : (lane + GROUP) * DH],
                     in_=y[:, qk].rearrange("p h s c -> p h (s c)"),
                 )
 
-        for k in range(GROUPS + 4):
-            if k < GROUPS:
-                sum_features(k)
-            if 0 <= k - 1 < GROUPS:
-                sum_squared_deviations(k - 1)
-            if 0 <= k - 2 < GROUPS:
-                normalise_and_transpose(k - 2)
-            if 0 <= k - 3 < GROUPS:
-                scale_shift_and_quantise(k - 3)
-            if k == 3:
-                for s in range(GROUP):
-                    for qk in range(2):
-                        project(0, s, qk)
-                project_plain(0)
-            if 0 <= k - 4 < GROUPS:
-                rotate_and_store(k - 4)
+        def exists(g):
+            return 0 <= g < GROUPS
+
+        for j in range(-2, GROUPS + 1):
+            if exists(j + 1):
+                normalise(j + 1)
+            if exists(j + 2):
+                sum_features(j + 2)
+            if j == -1:
+                half_sin = work.tile([P, 2, SLOTS, FREQS], F32)
+                nc.scalar.activation(out=half_sin[:], in_=rest[:], func=ACT.Sin, scale=math.pi)
+                w_codes, w_scales, plain_codes, plain_scales = quantise_weights(nc, keep, work, w_raw)
+                cos_tab, sin_tab = rotary_tables(nc, keep, work, half_sin)
+            if exists(j):
+                scale_shift_and_regroup(j)
+            if exists(j + 1):
+                transpose(j + 1)
+            if exists(j - 1):
+                multiply_by_tables(j - 1)
+            if exists(j):
+                quantise(j)
+                project(j)
+            if exists(j - 1):
+                add_and_store(j - 1)

@@ -187,7 +187,7 @@ def tile_transformerencoderlayer_pa_t_kernel(tc, x_grid, ln_g, ln_b, w_qk, out_0
         nc.vector.tensor_copy(out=gain_bias[:], in_=gb_columns[:, 0 : 2 * PACK])
 
         discard = keep.tile([P, D], BF16)
-        neg_means, z_tiles, zt_banks, xn_grouped, xn_operands = {}, {}, {}, {}, {}
+        neg_means, scales_shifts, z_tiles, zt_banks, xn_grouped, xn_operands = {}, {}, {}, {}, {}, {}
         u_banks, plain_banks, y_tiles, partner_tiles = {}, {}, {}, {}
 
         def sum_features(g):
@@ -202,7 +202,7 @@ def tile_transformerencoderlayer_pa_t_kernel(tc, x_grid, ln_g, ln_b, w_qk, out_0
             )
             neg_means[g] = neg_mean
 
-        def normalise(g):
+        def reciprocal_deviation(g):
             neg_mean = neg_means[g]
             squares = stats.tile([P, GROUP], F32)
             for s in range(GROUP):
@@ -218,11 +218,15 @@ def tile_transformerencoderlayer_pa_t_kernel(tc, x_grid, ln_g, ln_b, w_qk, out_0
             nc.gpsimd.tensor_tensor(out=rstd[:], in0=var_eps[:], in1=minus_half[:], op=ALU.pow)
             shift = stats.tile([P, GROUP], F32)
             nc.gpsimd.tensor_tensor(out=shift[:], in0=neg_mean[:], in1=rstd[:], op=ALU.mult)
+            scales_shifts[g] = (rstd, shift)
+
+        def normalise(g):
+            rstd, shift = scales_shifts[g]
             z = stage.tile([P, GROUP, D], F32)
             for s in range(GROUP):
-                nc.gpsimd.tensor_scalar(
-                    out=z[:, s], in0=x_sb[:, g, s], scalar1=rstd[:, s : s + 1],
-                    scalar2=shift[:, s : s + 1], op0=ALU.mult, op1=ALU.add,
+                nc.scalar.activation(
+                    out=z[:, s], in_=x_sb[:, g, s], func=ACT.Identity,
+                    scale=rstd[:, s : s + 1], bias=shift[:, s : s + 1],
                 )
             z_tiles[g] = z
 
@@ -342,9 +346,11 @@ def tile_transformerencoderlayer_pa_t_kernel(tc, x_grid, ln_g, ln_b, w_qk, out_0
 
         for j in range(-2, GROUPS + 1):
             if exists(j + 1):
-                normalise(j + 1)
+                reciprocal_deviation(j + 1)
             if exists(j + 2):
                 sum_features(j + 2)
+            if exists(j + 1):
+                normalise(j + 1)
             if j == -1:
                 half_sin = work.tile([P, 2, SLOTS, FREQS], F32)
                 nc.scalar.activation(out=half_sin[:], in_=rest[:], func=ACT.Sin, scale=math.pi)

import math
from contextlib import ExitStack

import concourse.masks as masks
import concourse.mybir as mybir

F32 = mybir.dt.float32
BF16 = mybir.dt.bfloat16
I32 = mybir.dt.int32
U32 = mybir.dt.uint32
U8 = mybir.dt.uint8
FP8X4 = mybir.dt.float8_e4m3fn_x4
ALU = mybir.AluOpType
ACT = mybir.ActivationFunctionType

P = 128
PACK = 4
D = P * PACK
TOKENS = 4096
GRID = 64
HEADS = 2
DH = 256
INNER = HEADS * DH
ROT = 200
HALF = ROT // 2
FREQS = HALF // 2
PLAIN = DH - ROT
EPS = 1e-5

BLOCKS = 4
LANES = 8
GROUP = 2
GROUPS = BLOCKS * LANES // GROUP
GROUP_TOKENS = GROUP * P
SLOTS = BLOCKS + LANES

FLOPS = 2 * TOKENS * D * 2 * INNER


def rotary_turns(nc, work):
    part = work.tile([P, 1], I32)
    nc.gpsimd.iota(part[:], pattern=[[0, 1]], base=0, channel_multiplier=1)
    offsets = work.tile([P, SLOTS], I32)
    nc.gpsimd.iota(offsets[:, 0:BLOCKS], pattern=[[GRID // BLOCKS, BLOCKS]], base=0, channel_multiplier=0)
    nc.gpsimd.iota(offsets[:, BLOCKS:SLOTS], pattern=[[1, LANES]], base=0, channel_multiplier=0)
    row_base = work.tile([P, 1], I32)
    nc.vector.tensor_single_scalar(out=row_base[:], in_=part[:], scalar=3, op=ALU.arith_shift_right)
    col_base = work.tile([P, 1], I32)
    nc.vector.tensor_scalar(
        out=col_base[:], in0=part[:], scalar1=7, scalar2=3,
        op0=ALU.bitwise_and, op1=ALU.logical_shift_left,
    )
    half_t = work.tile([P, SLOTS], F32)
    nc.vector.tensor_scalar(
        out=half_t[:, 0:BLOCKS], in0=offsets[:, 0:BLOCKS], scalar1=row_base[:, 0:1],
        scalar2=1.0 / (GRID - 1), op0=ALU.add, op1=ALU.mult,
    )
    nc.vector.tensor_scalar(
        out=half_t[:, BLOCKS:SLOTS], in0=offsets[:, BLOCKS:SLOTS], scalar1=col_base[:, 0:1],
        scalar2=1.0 / (GRID - 1), op0=ALU.add, op1=ALU.mult,
    )
    nc.vector.tensor_scalar_add(out=half_t[:], in0=half_t[:], scalar1=-0.5)

    beta = work.tile([P, FREQS], F32)
    nc.vector.memset(beta[:, 0:1], 1.0)
    ratio = 5.0 ** (1.0 / (FREQS - 1))
    have = 1
    while have < FREQS:
        more = min(have, FREQS - have)
        nc.vector.tensor_scalar_mul(
            out=beta[:, have : have + more], in0=beta[:, 0:more], scalar1=ratio**have
        )
        have += more

    shape = [P, SLOTS, FREQS]
    turns = work.tile([P, 2, SLOTS, FREQS], F32)
    nc.vector.tensor_tensor(
        out=turns[:, 0], in0=half_t[:].unsqueeze(2).to_broadcast(shape),
        in1=beta[:].unsqueeze(1).to_broadcast(shape), op=ALU.mult,
    )
    nc.vector.tensor_scalar_add(out=turns[:, 1], in0=turns[:, 0], scalar1=-0.25)
    whole = work.tile([P, 2, SLOTS, FREQS], I32)
    nc.vector.tensor_copy(out=whole[:], in_=turns[:])
    rest = work.tile([P, 2, SLOTS, FREQS], F32)
    nc.vector.tensor_tensor(out=rest[:], in0=turns[:], in1=whole[:], op=ALU.subtract)
    return rest


def rotary_tables(nc, keep, work, half_sin):
    square = work.tile([P, 2, SLOTS, FREQS], F32)
    nc.vector.tensor_tensor(out=square[:], in0=half_sin[:], in1=half_sin[:], op=ALU.mult)
    cos_tab = keep.tile([P, SLOTS, HALF], F32)
    sin_tab = keep.tile([P, SLOTS, HALF], F32)

    def finish(table_slots, squares, sign):
        count = squares.shape[1]
        nc.vector.tensor_scalar(
            out=table_slots.rearrange("p s (j e) -> p s j e", e=2),
            in0=squares.unsqueeze(3).to_broadcast([P, count, FREQS, 2]),
            scalar1=-2.0 * sign, scalar2=sign, op0=ALU.mult, op1=ALU.add,
        )

    finish(cos_tab[:], square[:, 0], 1.0)
    finish(sin_tab[:, 0:LANES], square[:, 1, BLOCKS:SLOTS], 1.0)
    finish(sin_tab[:, LANES:SLOTS], square[:, 1, 0:BLOCKS], -1.0)
    return cos_tab, sin_tab


def quantise_weights(nc, keep, work, raw):
    cols = 2 * INNER
    grouped = work.tile([P, cols, PACK], BF16, align_bytes=64)
    nc.vector.tensor_copy(out=grouped[:], in_=raw[:].rearrange("p t n -> p n t"))
    codes = keep.tile([P, cols], U32, align_bytes=64)
    scales = keep.tile([P, cols], U8, align_bytes=64)
    plain_grouped = work.tile([P, DH, PACK], BF16, align_bytes=64)
    nc.vector.memset(plain_grouped[:], 0.0)
    nc.vector.tensor_copy(
        out=plain_grouped[:, 0 : 2 * HEADS * PLAIN, :].rearrange("p (g c) t -> p g c t", c=PLAIN),
        in_=raw[:].rearrange("p t (g c) -> p g c t", c=DH)[:, :, ROT:DH, :],
    )
    nc.vector.quantize_mx(
        out=codes[:].bitcast(FP8X4), scales=scales[:], in_=grouped[:].rearrange("p n t -> p (n t)")
    )
    plain_codes = keep.tile([P, DH], U32, align_bytes=64)
    plain_scales = keep.tile([P, DH], U8, align_bytes=64)
    nc.vector.quantize_mx(
        out=plain_codes[:].bitcast(FP8X4), scales=plain_scales[:],
        in_=plain_grouped[:].rearrange("p n t -> p (n t)"),
    )
    return codes, scales, plain_codes, plain_scales


def tile_transformerencoderlayer_pa_t_kernel(tc, x_grid, ln_g, ln_b, w_qk, out_0, out_1):
    nc = tc.nc
    x_view = x_grid.rearrange("o (a p l) k -> p (o a) (l k)", a=BLOCKS, p=P, l=LANES)
    out_views = [
        out.rearrange("o h (a p l) c -> p (o h) a (l c)", a=BLOCKS, p=P, l=LANES)
        for out in (out_0, out_1)
    ]

    with ExitStack() as ctx:
        keep = ctx.enter_context(tc.tile_pool(name="keep", bufs=1))
        work = ctx.enter_context(tc.tile_pool(name="work", bufs=1))
        stats = ctx.enter_context(tc.tile_pool(name="stats", bufs=4))
        stage = ctx.enter_context(tc.tile_pool(name="stage", bufs=3))
        results = ctx.enter_context(tc.tile_pool(name="results", bufs=3))
        zt_psum = ctx.enter_context(tc.psum_pool(name="zt_psum", bufs=2))
        u_psum = ctx.enter_context(tc.psum_pool(name="u_psum", bufs=4))
        plain_psum = ctx.enter_context(tc.psum_pool(name="plain_psum", bufs=2))
        ctx.enter_context(tc.manual_schedule())

        def block_and_lane(g):
            return g // (LANES // GROUP), GROUP * (g % (LANES // GROUP))

        x_sb = keep.tile([P, GROUPS, GROUP, D], BF16)

        def load_x(g):
            a, lane = block_and_lane(g)
            nc.sync.dma_start(
                out=x_sb[:, g].rearrange("p s k -> p (s k)"),
                in_=x_view[:, a, lane * D : (lane + GROUP) * D],
            )

        gb_rows = work.tile([P, P], BF16)
        nc.vector.memset(gb_rows[:], 0.0)
        w_raw = work.tile([P, PACK, 2 * INNER], BF16)
        load_x(0)
        nc.sync.dma_start(out=gb_rows[0:PACK, :], in_=ln_g.rearrange("(t p) -> t p", p=P))
        nc.sync.dma_start(out=gb_rows[PACK : 2 * PACK, :], in_=ln_b.rearrange("(t p) -> t p", p=P))
        load_x(1)
        nc.sync.dma_start(out=w_raw[:], in_=w_qk.rearrange("(t p) n -> p t n", p=P))
        for g in range(2, GROUPS):
            load_x(g)

        minus_half = keep.tile([P, GROUP], F32)
        nc.vector.memset(minus_half[:], -0.5)
        warm = work.tile([P, 1], F32)
        nc.scalar.activation(out=warm[:], in_=minus_half[:, 0:1], func=ACT.Sin)
        rest = rotary_turns(nc, work)
        ident = keep.tile([P, P], F32)
        masks.make_identity(nc, ident[:])
        gb_rows32 = work.tile([P, P], F32)
        nc.vector.tensor_copy(out=gb_rows32[:], in_=gb_rows[:])
        gb_columns = zt_psum.tile([P, P], F32, tag="zt")
        nc.tensor.transpose(out=gb_columns[:], in_=gb_rows32[:], identity=ident[:])
        gain_bias = keep.tile([P, 2 * PACK], F32)
        nc.vector.tensor_copy(out=gain_bias[:], in_=gb_columns[:, 0 : 2 * PACK])

        discard = keep.tile([P, D], BF16)
        neg_means, scales_shifts, z_tiles, zt_banks, xn_grouped, xn_operands = {}, {}, {}, {}, {}, {}
        u_banks, plain_banks, y_tiles, partner_tiles = {}, {}, {}, {}

        def sum_features(g):
            total = stats.tile([P, GROUP], F32)
            for s in range(GROUP):
                nc.scalar.activation(
                    out=discard[:], in_=x_sb[:, g, s], func=ACT.Copy, accum_out=total[:, s : s + 1]
                )
            neg_mean = stats.tile([P, GROUP], F32)
            nc.gpsimd.tensor_scalar(
                out=neg_mean[:], in0=total[:], scalar1=-1.0 / D, scalar2=0.0, op0=ALU.mult, op1=ALU.add
            )
            neg_means[g] = neg_mean

        def reciprocal_deviation(g):
            neg_mean = neg_means[g]
            squares = stats.tile([P, GROUP], F32)
            for s in range(GROUP):
                nc.scalar.activation(
                    out=discard[:], in_=x_sb[:, g, s], func=ACT.Square,
                    bias=neg_mean[:, s : s + 1], accum_out=squares[:, s : s + 1],
                )
            var_eps = stats.tile([P, GROUP], F32)
            nc.gpsimd.tensor_scalar(
                out=var_eps[:], in0=squares[:], scalar1=1.0 / D, scalar2=EPS, op0=ALU.mult, op1=ALU.add
            )
            rstd = stats.tile([P, GROUP], F32)
            nc.gpsimd.tensor_tensor(out=rstd[:], in0=var_eps[:], in1=minus_half[:], op=ALU.pow)
            shift = stats.tile([P, GROUP], F32)
            nc.gpsimd.tensor_tensor(out=shift[:], in0=neg_mean[:], in1=rstd[:], op=ALU.mult)
            scales_shifts[g] = (rstd, shift)

        def normalise(g):
            rstd, shift = scales_shifts[g]
            z = stage.tile([P, GROUP, D], F32)
            for s in range(GROUP):
                nc.scalar.activation(
                    out=z[:, s], in_=x_sb[:, g, s], func=ACT.Identity,
                    scale=rstd[:, s : s + 1], bias=shift[:, s : s + 1],
                )
            z_tiles[g] = z

        def transpose(g):
            z = z_tiles[g]
            banks = []
            for half in range(2):
                zt = zt_psum.tile([P, 2, GROUP_TOKENS], F32, tag="zt")
                for i in range(2):
                    t = 2 * half + i
                    for s in range(GROUP):
                        nc.tensor.transpose(
                            out=zt[:, i, s * P : (s + 1) * P], in_=z[:, s, t * P : (t + 1) * P],
                            identity=ident[:],
                        )
                banks.append(zt)
            zt_banks[g] = banks

        def scale_shift_and_regroup(g):
            planes = stage.tile([P, PACK, GROUP_TOKENS], BF16)
            for half in range(2):
                for i in range(2):
                    t = 2 * half + i
                    nc.scalar.activation(
                        out=planes[:, t], in_=zt_banks[g][half][:, i], func=ACT.Identity,
                        scale=gain_bias[:, t : t + 1], bias=gain_bias[:, PACK + t : PACK + t + 1],
                    )
            grouped = stage.tile([P, GROUP_TOKENS, PACK], BF16, align_bytes=64)
            nc.scalar.copy(out=grouped[:], in_=planes[:].rearrange("p t w -> p w t"))
            xn_grouped[g] = grouped

        def quantise(g):
            codes = stage.tile([P, GROUP_TOKENS], U32, align_bytes=64)
            scales = stage.tile([P, GROUP_TOKENS], U8, align_bytes=64)
            nc.vector.quantize_mx(
                out=codes[:].bitcast(FP8X4), scales=scales[:],
                in_=xn_grouped[g][:].rearrange("p w t -> p (w t)"),
            )
            xn_operands[g] = (codes, scales)

        def project(g):
            codes, scales = xn_operands[g]
            for s in range(GROUP):
                tokens = slice(s * P, (s + 1) * P)
                for qk in range(2):
                    columns = slice(qk * INNER, (qk + 1) * INNER)
                    u = u_psum.tile([P, INNER], F32)
                    nc.tensor.matmul_mx(
                        out=u[:],
                        lhsT=codes[:, tokens].bitcast(FP8X4), lhsT_scale=scales[:, tokens],
                        rhs=w_codes[:, columns].bitcast(FP8X4), rhs_scale=w_scales[:, columns],
                        start=True, stop=True,
                    )
                    u_banks[(g, s, qk)] = u
            plain = plain_psum.tile([P, GROUP, DH], F32)
            for s in range(GROUP):
                tokens = slice(s * P, (s + 1) * P)
                nc.tensor.matmul_mx(
                    out=plain[:, s],
                    lhsT=codes[:, tokens].bitcast(FP8X4), lhsT_scale=scales[:, tokens],
                    rhs=plain_codes[:].bitcast(FP8X4), rhs_scale=plain_scales[:],
                    start=True, stop=True,
                )
            plain_banks[g] = plain

        def multiply_by_tables(g):
            a, lane = block_and_lane(g)
            y = results.tile([P, 2, HEADS, GROUP, DH], F32)
            partner = results.tile([P, 2, HEADS, GROUP, ROT], F32)
            both_heads = [P, HEADS, 2, HALF]
            for s in range(GROUP):
                l = lane + s
                cosines = cos_tab[:, a : BLOCKS + l + 1 : BLOCKS + l - a]
                sines = sin_tab[:, l : LANES + a + 1 : LANES + a - l]
                for qk in range(2):
                    u = u_banks[(g, s, qk)][:].rearrange("p (h c) -> p h c", h=HEADS)[:, :, 0:ROT]
                    nc.vector.tensor_tensor(
                        out=y[:, qk, :, s, 0:ROT].rearrange("p h (f c) -> p h f c", f=2),
                        in0=u.rearrange("p h (f c) -> p h f c", f=2),
                        in1=cosines.unsqueeze(1).to_broadcast(both_heads),
                        op=ALU.mult,
                    )
                    nc.vector.tensor_tensor(
                        out=partner[:, qk, :, s].rearrange("p h (e i) -> p h e i", e=2),
                        in0=u.rearrange("p h (i e) -> p h e i", e=2),
                        in1=sines.unsqueeze(1).to_broadcast(both_heads),
                        op=ALU.mult,
                    )
            y_tiles[g] = y
            partner_tiles[g] = partner

        def add_and_store(g):
            a, lane = block_and_lane(g)
            y = y_tiles[g]
            y_rows = y[:].rearrange("p q h s c -> p (q h s) c")
            partner_rows = partner_tiles[g][:].rearrange("p q h s c -> p (q h s) c")
            nc.vector.tensor_tensor(
                out=y_rows[:, :, HALF:ROT], in0=y_rows[:, :, HALF:ROT],
                in1=partner_rows[:, :, 0:HALF], op=ALU.add,
            )
            nc.vector.tensor_tensor(
                out=y_rows[:, :, 0:HALF], in0=y_rows[:, :, 0:HALF],
                in1=partner_rows[:, :, HALF:ROT], op=ALU.add,
            )
            nc.scalar.copy(
                out=y[:].rearrange("p q h s c -> p s (q h) c")[:, :, :, ROT:DH],
                in_=plain_banks[g][:, :, 0 : 2 * HEADS * PLAIN].rearrange("p s (g c) -> p s g c", c=PLAIN),
            )
            for qk in range(2):
                nc.sync.dma_start(
                    out=out_views[qk][:, :, a, lane * DH : (lane + GROUP) * DH],
                    in_=y[:, qk].rearrange("p h s c -> p h (s c)"),
                )

        def exists(g):
            return 0 <= g < GROUPS

        for j in range(-2, GROUPS + 1):
            if exists(j + 1):
                reciprocal_deviation(j + 1)
            if exists(j + 2):
                sum_features(j + 2)
            if exists(j + 1):
                normalise(j + 1)
            if j == -1:
                half_sin = work.tile([P, 2, SLOTS, FREQS], F32)
                nc.scalar.activation(out=half_sin[:], in_=rest[:], func=ACT.Sin, scale=math.pi)
                w_codes, w_scales, plain_codes, plain_scales = quantise_weights(nc, keep, work, w_raw)
                cos_tab, sin_tab = rotary_tables(nc, keep, work, half_sin)
            if exists(j):
                scale_shift_and_regroup(j)
            if exists(j + 1):
                transpose(j + 1)
            if exists(j - 1):
                multiply_by_tables(j - 1)
            if exists(j):
                quantise(j)
                project(j)
            if exists(j - 1):
                add_and_store(j - 1)
